import numpy as np
import ml_dtypes

BF16 = ml_dtypes.bfloat16


def bf(x):
    return np.asarray(x, np.float32).astype(BF16)


def f32(x):
    return np.asarray(x, np.float32)


def f64(x):
    return np.asarray(x).astype(np.float64)


def striped(idx):
    return np.tile(idx.reshape(-1, 16).T, (8, 1))


C, S, N, DIM = 256, 512, 256, 2


def setup_inputs():
    pts = np.random.rand(N, DIM)
    dist = np.sqrt(np.square(pts[:, None, :] - pts[None, :, :]).sum(axis=-1))
    w1 = np.where(np.random.rand(C, 1) < 0.5, -1.0, 1.0) * (0.75 + 0.5 * np.random.rand(C, 1))
    return {"base": f32(np.random.standard_normal((C, S))), "state": f32(np.random.standard_normal((1, N))), "dist": f32(dist), "w1": f32(w1), "w4": f32(0.05 * np.random.standard_normal((C, 1))), "b4": f32(0.025 * np.random.standard_normal((C, 1))), "w3": bf(0.5 * np.random.standard_normal((C, C)) / N), "bias": f32(0.2 * np.random.standard_normal((C, 1))), "offs": striped(np.random.permutation(S)[:N])}


def reference(base, state, dist, w1, w4, b4, w3, bias, offs):
    idx = offs[:16].T.reshape(-1)
    d = f64(dist)
    a4 = f64(w4)
    c4 = f64(b4)
    msg = np.stack([np.maximum(d * a4[h, 0] + c4[h, 0], 0.0).sum(axis=1) for h in range(C)])
    emb = np.maximum(f64(w1) * f64(state) + f64(w3).T @ msg + f64(bias), 0.0)
    mean = emb.sum(axis=1, keepdims=True) / N
    std = np.sqrt(np.square(emb - mean).sum(axis=1, keepdims=True) / (N - 1))
    out = f64(base).copy()
    out[:, idx] = (emb - mean) * (1.0 / std)
    return out

@@ -1,0 +1,119 @@
+import concourse.mybir as mybir
+from concourse.masks import make_identity
+
+F32, BF16, U16 = mybir.dt.float32, mybir.dt.bfloat16, mybir.dt.uint16
+ACT = mybir.ActivationFunctionType
+ALU = mybir.AluOpType
+
+P = 128
+C = 256
+N = 256
+S = 512
+BLOCKS = 2
+
+FLOPS = 4 * C * N * N + 2 * C * C * N
+
+
+def tile_s2v_dqn_kernel(tc, base, state, dist, w1, w4, b4, w3, bias, offs, out):
+    nc = tc.nc
+    with (
+        tc.tile_pool(name="held", bufs=1) as held,
+        tc.tile_pool(name="unread", bufs=4) as unread,
+        tc.tile_pool(name="work", bufs=2) as work,
+        tc.psum_pool(name="psum", bufs=2) as psum,
+    ):
+        offsets = held.tile([P, N // 16], U16, name="offsets")
+        nc.sync.dma_start(offsets[:], offs)
+
+        dist_rows = [held.tile([P, N], F32, name=f"dist_rows{jb}") for jb in range(BLOCKS)]
+        for jb in range(BLOCKS):
+            nc.sync.dma_start(dist_rows[jb][:], dist[jb * P : (jb + 1) * P, :])
+
+        slope = held.tile([P, C], F32, name="slope")
+        nc.scalar.dma_start(slope[:], w4.rearrange("h o -> (h o)").partition_broadcast(P))
+        shift = held.tile([P, C], F32, name="shift")
+        nc.gpsimd.dma_start(shift[:], b4.rearrange("h o -> (h o)").partition_broadcast(P))
+        neg_shift = held.tile([P, C], F32, name="neg_shift")
+        nc.vector.tensor_scalar_mul(neg_shift[:], shift[:], -1.0)
+
+        identity = held.tile([P, P], F32, name="identity")
+        make_identity(nc, identity[:])
+        ones = held.tile([P, N], F32, name="ones")
+        nc.gpsimd.memset(ones[:], 1.0)
+
+        own_weights = held.tile([2, C], F32, name="own_weights")
+        nc.sync.dma_start(own_weights[0:1, :], bias.rearrange("c o -> o c"))
+        nc.sync.dma_start(own_weights[1:2, :], w1.rearrange("c o -> o c"))
+        own_rows = held.tile([2, N], F32, name="own_rows")
+        nc.vector.memset(own_rows[0:1, :], 1.0)
+        nc.sync.dma_start(own_rows[1:2, :], state)
+
+        w3_rows = [held.tile([P, C], BF16, name=f"w3_rows{hb}") for hb in range(BLOCKS)]
+        for hb in range(BLOCKS):
+            nc.sync.dma_start(w3_rows[hb][:], w3[hb * P : (hb + 1) * P, :])
+        window = [held.tile([P, S], F32, name=f"window{cb}") for cb in range(BLOCKS)]
+        for cb in range(BLOCKS):
+            nc.sync.dma_start(window[cb][:], base[cb * P : (cb + 1) * P, :])
+
+        msg = [held.tile([P, N], BF16, name=f"msg{hb}") for hb in range(BLOCKS)]
+
+        for jb in range(BLOCKS):
+            msg_by_node = held.tile([P, C], F32, name=f"msg_by_node{jb}")
+            clipped_sum = held.tile([P, P], F32, name=f"clipped_sum{jb}")
+            for i in range(P):
+                h = i
+                relu_terms = unread.tile([P, N], F32, name="relu_terms")
+                nc.scalar.activation(
+                    relu_terms[:],
+                    dist_rows[jb][:],
+                    ACT.Relu,
+                    bias=shift[:, h : h + 1],
+                    scale=slope[:, h : h + 1],
+                    accum_out=msg_by_node[:, h : h + 1],
+                )
+                h = P + i
+                clipped_terms = unread.tile([P, N], F32, name="clipped_terms")
+                nc.vector.scalar_tensor_tensor(
+                    clipped_terms[:],
+                    dist_rows[jb][:],
+                    slope[:, h : h + 1],
+                    neg_shift[:, h : h + 1].to_broadcast([P, N]),
+                    ALU.mult,
+                    ALU.max,
+                    accum_out=clipped_sum[:, i : i + 1],
+                )
+            nc.vector.scalar_tensor_tensor(
+                msg_by_node[:, P:C], shift[:, P:C], float(N), clipped_sum[:], ALU.mult, ALU.add
+            )
+            for hb in range(BLOCKS):
+                flipped = psum.tile([P, P], F32, name="flipped")
+                nc.tensor.transpose(flipped[:], msg_by_node[:, hb * P : (hb + 1) * P], identity[:])
+                nc.vector.tensor_copy(msg[hb][:, jb * P : (jb + 1) * P], flipped[:])
+
+        for cb in range(BLOCKS):
+            channels = slice(cb * P, (cb + 1) * P)
+            emb_sum = psum.tile([P, N], F32, name="emb_sum")
+            nc.tensor.matmul(emb_sum[:], own_weights[:, channels], own_rows[:], start=True, stop=False)
+            nc.tensor.matmul(emb_sum[:], w3_rows[0][:, channels], msg[0][:], start=False, stop=False)
+            nc.tensor.matmul(emb_sum[:], w3_rows[1][:, channels], msg[1][:], start=False, stop=True)
+
+            emb = work.tile([P, N], F32, name="emb")
+            total = work.tile([P, 1], F32, name="total")
+            nc.scalar.activation(emb[:], emb_sum[:], ACT.Relu, accum_out=total[:])
+            neg_mean = work.tile([P, 1], F32, name="neg_mean")
+            nc.vector.tensor_scalar_mul(neg_mean[:], total[:], -1.0 / N)
+            centered = work.tile([P, N], F32, name="centered")
+            nc.vector.tensor_scalar_add(centered[:], emb[:], neg_mean[:])
+            squares = work.tile([P, N], F32, name="squares")
+            square_sum = work.tile([P, 1], F32, name="square_sum")
+            nc.scalar.activation(squares[:], emb[:], ACT.Square, bias=neg_mean[:], accum_out=square_sum[:])
+            std = work.tile([P, 1], F32, name="std")
+            nc.scalar.activation(std[:], square_sum[:], ACT.Sqrt, scale=1.0 / (N - 1))
+            inv_std = work.tile([P, 1], F32, name="inv_std")
+            nc.vector.reciprocal(inv_std[:], std[:])
+
+            inv_std_wide = work.tile([P, N], F32, name="inv_std_wide")
+            nc.vector.tensor_scalar_mul(inv_std_wide[:], ones[:], inv_std[:])
+
+            nc.vector.tensor_tensor(window[cb][:].indirect(offsets[:]), centered[:], inv_std_wide[:], ALU.mult)
+            nc.sync.dma_start(out[channels, :], window[cb][:])

@@ -10,6 +10,8 @@ C = 256
 N = 256
 S = 512
 BLOCKS = 2
+H_SCALAR = 96
+H_VECTOR = C - H_SCALAR
 
 FLOPS = 4 * C * N * N + 2 * C * C * N
 
@@ -59,9 +61,8 @@ def tile_s2v_dqn_kernel(tc, base, state, dist, w1, w4, b4, w3, bias, offs, out):
 
         for jb in range(BLOCKS):
             msg_by_node = held.tile([P, C], F32, name=f"msg_by_node{jb}")
-            clipped_sum = held.tile([P, P], F32, name=f"clipped_sum{jb}")
-            for i in range(P):
-                h = i
+            clipped_sum = held.tile([P, H_VECTOR], F32, name=f"clipped_sum{jb}")
+            for h in range(H_SCALAR):
                 relu_terms = unread.tile([P, N], F32, name="relu_terms")
                 nc.scalar.activation(
                     relu_terms[:],
@@ -71,7 +72,7 @@ def tile_s2v_dqn_kernel(tc, base, state, dist, w1, w4, b4, w3, bias, offs, out):
                     scale=slope[:, h : h + 1],
                     accum_out=msg_by_node[:, h : h + 1],
                 )
-                h = P + i
+            for h in range(H_SCALAR, C):
                 clipped_terms = unread.tile([P, N], F32, name="clipped_terms")
                 nc.vector.scalar_tensor_tensor(
                     clipped_terms[:],
@@ -80,10 +81,10 @@ def tile_s2v_dqn_kernel(tc, base, state, dist, w1, w4, b4, w3, bias, offs, out):
                     neg_shift[:, h : h + 1].to_broadcast([P, N]),
                     ALU.mult,
                     ALU.max,
-                    accum_out=clipped_sum[:, i : i + 1],
+                    accum_out=clipped_sum[:, h - H_SCALAR : h - H_SCALAR + 1],
                 )
             nc.vector.scalar_tensor_tensor(
-                msg_by_node[:, P:C], shift[:, P:C], float(N), clipped_sum[:], ALU.mult, ALU.add
+                msg_by_node[:, H_SCALAR:C], shift[:, H_SCALAR:C], float(N), clipped_sum[:], ALU.mult, ALU.add
             )
             for hb in range(BLOCKS):
                 flipped = psum.tile([P, P], F32, name="flipped")

@@ -10,7 +10,7 @@ C = 256
 N = 256
 S = 512
 BLOCKS = 2
-H_SCALAR = 96
+H_SCALAR = 160
 H_VECTOR = C - H_SCALAR
 
 FLOPS = 4 * C * N * N + 2 * C * C * N

@@ -10,8 +10,12 @@ C = 256
 N = 256
 S = 512
 BLOCKS = 2
-H_SCALAR = 160
-H_VECTOR = C - H_SCALAR
+
+H_TENSOR = 68
+H_VECTOR = H_TENSOR
+H_SCALAR = C - H_VECTOR - H_TENSOR
+assert H_TENSOR <= P
+assert H_SCALAR % 8 == 0
 
 FLOPS = 4 * C * N * N + 2 * C * C * N
 
@@ -21,8 +25,10 @@ def tile_s2v_dqn_kernel(tc, base, state, dist, w1, w4, b4, w3, bias, offs, out):
     with (
         tc.tile_pool(name="held", bufs=1) as held,
         tc.tile_pool(name="unread", bufs=4) as unread,
+        tc.tile_pool(name="ring", bufs=4) as ring,
         tc.tile_pool(name="work", bufs=2) as work,
         tc.psum_pool(name="psum", bufs=2) as psum,
+        tc.psum_pool(name="psum_held", bufs=1) as psum_held,
     ):
         offsets = held.tile([P, N // 16], U16, name="offsets")
         nc.sync.dma_start(offsets[:], offs)
@@ -42,6 +48,9 @@ def tile_s2v_dqn_kernel(tc, base, state, dist, w1, w4, b4, w3, bias, offs, out):
         make_identity(nc, identity[:])
         ones = held.tile([P, N], F32, name="ones")
         nc.gpsimd.memset(ones[:], 1.0)
+        one_column = held.tile([P, 2 * P - 1], F32, name="one_column")
+        nc.gpsimd.memset(one_column[:], 0.0)
+        nc.gpsimd.memset(one_column[:, P - 1 : P], 1.0)
 
         own_weights = held.tile([2, C], F32, name="own_weights")
         nc.sync.dma_start(own_weights[0:1, :], bias.rearrange("c o -> o c"))
@@ -57,11 +66,20 @@ def tile_s2v_dqn_kernel(tc, base, state, dist, w1, w4, b4, w3, bias, offs, out):
         for cb in range(BLOCKS):
             nc.sync.dma_start(window[cb][:], base[cb * P : (cb + 1) * P, :])
 
-        msg = [held.tile([P, N], BF16, name=f"msg{hb}") for hb in range(BLOCKS)]
+        dist_cols = held.tile([P, BLOCKS, N], F32, name="dist_cols")
+        for jb in range(BLOCKS):
+            for kb in range(BLOCKS):
+                flipped = psum.tile([P, P], F32, name="flipped")
+                nc.tensor.transpose(flipped[:], dist_rows[jb][:, kb * P : (kb + 1) * P], identity[:])
+                nc.vector.tensor_copy(dist_cols[:, kb, jb * P : (jb + 1) * P], flipped[:])
+
+        msg_by_node = [held.tile([P, C], F32, name=f"msg_by_node{jb}") for jb in range(BLOCKS)]
+        clipped_sum = [held.tile([P, C - H_SCALAR], F32, name=f"clipped_sum{jb}") for jb in range(BLOCKS)]
+        for jb in range(BLOCKS):
+            nc.gpsimd.memset(clipped_sum[jb][:], 0.0)
+        msg_sum = [psum_held.tile([P, N], F32, name=f"msg_sum{hb}") for hb in range(BLOCKS)]
 
         for jb in range(BLOCKS):
-            msg_by_node = held.tile([P, C], F32, name=f"msg_by_node{jb}")
-            clipped_sum = held.tile([P, H_VECTOR], F32, name=f"clipped_sum{jb}")
             for h in range(H_SCALAR):
                 relu_terms = unread.tile([P, N], F32, name="relu_terms")
                 nc.scalar.activation(
@@ -70,9 +88,26 @@ def tile_s2v_dqn_kernel(tc, base, state, dist, w1, w4, b4, w3, bias, offs, out):
                     ACT.Relu,
                     bias=shift[:, h : h + 1],
                     scale=slope[:, h : h + 1],
-                    accum_out=msg_by_node[:, h : h + 1],
+                    accum_out=msg_by_node[jb][:, h : h + 1],
                 )
-            for h in range(H_SCALAR, C):
+
+        vector_sums = [(jb, h) for jb in range(BLOCKS) for h in range(H_SCALAR, H_SCALAR + H_VECTOR)]
+        for turn in range(H_TENSOR):
+            h = C - H_TENSOR + turn
+            row = h - P
+            terms = ring.tile([P, BLOCKS, N], F32, name="terms")
+            nc.vector.tensor_scalar(
+                terms[:], dist_cols[:], slope[:, h : h + 1], neg_shift[:, h : h + 1], ALU.mult, ALU.max
+            )
+            for kb in range(BLOCKS):
+                nc.tensor.matmul(
+                    msg_sum[1][:],
+                    one_column[:, P - 1 - row : 2 * P - 1 - row],
+                    terms[:, kb, :],
+                    start=(turn == 0 and kb == 0),
+                    stop=False,
+                )
+            for jb, h in vector_sums[BLOCKS * turn : BLOCKS * (turn + 1)]:
                 clipped_terms = unread.tile([P, N], F32, name="clipped_terms")
                 nc.vector.scalar_tensor_tensor(
                     clipped_terms[:],
@@ -81,15 +116,20 @@ def tile_s2v_dqn_kernel(tc, base, state, dist, w1, w4, b4, w3, bias, offs, out):
                     neg_shift[:, h : h + 1].to_broadcast([P, N]),
                     ALU.mult,
                     ALU.max,
-                    accum_out=clipped_sum[:, h - H_SCALAR : h - H_SCALAR + 1],
+                    accum_out=clipped_sum[jb][:, h - H_SCALAR : h - H_SCALAR + 1],
                 )
+
+        for jb in range(BLOCKS):
+            nodes = slice(jb * P, (jb + 1) * P)
             nc.vector.scalar_tensor_tensor(
-                msg_by_node[:, H_SCALAR:C], shift[:, H_SCALAR:C], float(N), clipped_sum[:], ALU.mult, ALU.add
+                msg_by_node[jb][:, H_SCALAR:C], shift[:, H_SCALAR:C], float(N), clipped_sum[jb][:], ALU.mult, ALU.add
             )
-            for hb in range(BLOCKS):
-                flipped = psum.tile([P, P], F32, name="flipped")
-                nc.tensor.transpose(flipped[:], msg_by_node[:, hb * P : (hb + 1) * P], identity[:])
-                nc.vector.tensor_copy(msg[hb][:, jb * P : (jb + 1) * P], flipped[:])
+            nc.tensor.matmul(msg_sum[0][:, nodes], msg_by_node[jb][:, 0:P], identity[:], start=(jb == 0), stop=(jb == 1))
+            nc.tensor.matmul(msg_sum[1][:, nodes], msg_by_node[jb][:, P:C], identity[:], start=False, stop=(jb == 1))
+
+        msg = [held.tile([P, N], BF16, name=f"msg{hb}") for hb in range(BLOCKS)]
+        nc.scalar.copy(msg[0][:], msg_sum[0][:])
+        nc.vector.tensor_copy(msg[1][:], msg_sum[1][:])
 
         for cb in range(BLOCKS):
             channels = slice(cb * P, (cb + 1) * P)
@@ -112,7 +152,6 @@ def tile_s2v_dqn_kernel(tc, base, state, dist, w1, w4, b4, w3, bias, offs, out):
             nc.scalar.activation(std[:], square_sum[:], ACT.Sqrt, scale=1.0 / (N - 1))
             inv_std = work.tile([P, 1], F32, name="inv_std")
             nc.vector.reciprocal(inv_std[:], std[:])
-
             inv_std_wide = work.tile([P, N], F32, name="inv_std_wide")
             nc.vector.tensor_scalar_mul(inv_std_wide[:], ones[:], inv_std[:])
 

@@ -11,9 +11,9 @@ N = 256
 S = 512
 BLOCKS = 2
 
-H_TENSOR = 68
-H_VECTOR = H_TENSOR
-H_SCALAR = C - H_VECTOR - H_TENSOR
+H_SCALAR = 120
+H_VECTOR = 80
+H_TENSOR = C - H_SCALAR - H_VECTOR
 assert H_TENSOR <= P
 assert H_SCALAR % 8 == 0
 
@@ -107,7 +107,7 @@ def tile_s2v_dqn_kernel(tc, base, state, dist, w1, w4, b4, w3, bias, offs, out):
                     start=(turn == 0 and kb == 0),
                     stop=False,
                 )
-            for jb, h in vector_sums[BLOCKS * turn : BLOCKS * (turn + 1)]:
+            for jb, h in vector_sums[len(vector_sums) * turn // H_TENSOR : len(vector_sums) * (turn + 1) // H_TENSOR]:
                 clipped_terms = unread.tile([P, N], F32, name="clipped_terms")
                 nc.vector.scalar_tensor_tensor(
                     clipped_terms[:],

@@ -14,8 +14,8 @@ BLOCKS = 2
 H_SCALAR = 120
 H_VECTOR = 80
 H_TENSOR = C - H_SCALAR - H_VECTOR
-assert H_TENSOR <= P
-assert H_SCALAR % 8 == 0
+assert H_SCALAR % 8 == 0 and H_VECTOR % 8 == 0
+assert H_TENSOR <= P and H_TENSOR % BLOCKS == 0
 
 FLOPS = 4 * C * N * N + 2 * C * C * N
 
@@ -41,8 +41,10 @@ def tile_s2v_dqn_kernel(tc, base, state, dist, w1, w4, b4, w3, bias, offs, out):
         nc.scalar.dma_start(slope[:], w4.rearrange("h o -> (h o)").partition_broadcast(P))
         shift = held.tile([P, C], F32, name="shift")
         nc.gpsimd.dma_start(shift[:], b4.rearrange("h o -> (h o)").partition_broadcast(P))
-        neg_shift = held.tile([P, C], F32, name="neg_shift")
-        nc.vector.tensor_scalar_mul(neg_shift[:], shift[:], -1.0)
+
+        scratch = held.tile([P, 1], F32, name="scratch")
+        nc.vector.memset(scratch[:], 1.0)
+        nc.scalar.activation(scratch[:], scratch[:], ACT.Sqrt)
 
         identity = held.tile([P, P], F32, name="identity")
         make_identity(nc, identity[:])
@@ -51,6 +53,15 @@ def tile_s2v_dqn_kernel(tc, base, state, dist, w1, w4, b4, w3, bias, offs, out):
         one_column = held.tile([P, 2 * P - 1], F32, name="one_column")
         nc.gpsimd.memset(one_column[:], 0.0)
         nc.gpsimd.memset(one_column[:, P - 1 : P], 1.0)
+
+        b4_row = held.tile([1, C], F32, name="b4_row")
+        nc.sync.dma_start(b4_row[:], b4.rearrange("h o -> o h"))
+        minus_ones = held.tile([1, P], F32, name="minus_ones")
+        nc.vector.memset(minus_ones[:], -1.0)
+        neg_shift = psum_held.tile([P, C], F32, name="neg_shift")
+        nc.tensor.matmul(neg_shift[:], minus_ones[:], b4_row[:], start=True, stop=True)
+        neg_shift_sbuf = held.tile([P, C], F32, name="neg_shift_sbuf")
+        nc.vector.tensor_scalar_mul(neg_shift_sbuf[:], shift[:], -1.0)
 
         own_weights = held.tile([2, C], F32, name="own_weights")
         nc.sync.dma_start(own_weights[0:1, :], bias.rearrange("c o -> o c"))
@@ -73,13 +84,12 @@ def tile_s2v_dqn_kernel(tc, base, state, dist, w1, w4, b4, w3, bias, offs, out):
                 nc.tensor.transpose(flipped[:], dist_rows[jb][:, kb * P : (kb + 1) * P], identity[:])
                 nc.vector.tensor_copy(dist_cols[:, kb, jb * P : (jb + 1) * P], flipped[:])
 
-        msg_by_node = [held.tile([P, C], F32, name=f"msg_by_node{jb}") for jb in range(BLOCKS)]
-        clipped_sum = [held.tile([P, C - H_SCALAR], F32, name=f"clipped_sum{jb}") for jb in range(BLOCKS)]
-        for jb in range(BLOCKS):
-            nc.gpsimd.memset(clipped_sum[jb][:], 0.0)
         msg_sum = [psum_held.tile([P, N], F32, name=f"msg_sum{hb}") for hb in range(BLOCKS)]
 
         for jb in range(BLOCKS):
+            nodes = slice(jb * P, (jb + 1) * P)
+            msg_by_node = held.tile([P, C], F32, name=f"msg_by_node{jb}")
+
             for h in range(H_SCALAR):
                 relu_terms = unread.tile([P, N], F32, name="relu_terms")
                 nc.scalar.activation(
@@ -88,44 +98,45 @@ def tile_s2v_dqn_kernel(tc, base, state, dist, w1, w4, b4, w3, bias, offs, out):
                     ACT.Relu,
                     bias=shift[:, h : h + 1],
                     scale=slope[:, h : h + 1],
-                    accum_out=msg_by_node[jb][:, h : h + 1],
+                    accum_out=msg_by_node[:, h : h + 1],
                 )
 
-        vector_sums = [(jb, h) for jb in range(BLOCKS) for h in range(H_SCALAR, H_SCALAR + H_VECTOR)]
-        for turn in range(H_TENSOR):
-            h = C - H_TENSOR + turn
-            row = h - P
-            terms = ring.tile([P, BLOCKS, N], F32, name="terms")
-            nc.vector.tensor_scalar(
-                terms[:], dist_cols[:], slope[:, h : h + 1], neg_shift[:, h : h + 1], ALU.mult, ALU.max
-            )
-            for kb in range(BLOCKS):
-                nc.tensor.matmul(
-                    msg_sum[1][:],
-                    one_column[:, P - 1 - row : 2 * P - 1 - row],
-                    terms[:, kb, :],
-                    start=(turn == 0 and kb == 0),
-                    stop=False,
+            clipped_sum = held.tile([P, C - H_SCALAR], F32, name=f"clipped_sum{jb}")
+            nc.gpsimd.memset(clipped_sum[:, H_VECTOR:], 0.0)
+            turns = H_TENSOR // BLOCKS
+            for turn in range(turns):
+                h = C - H_TENSOR + jb * turns + turn
+                row = h - P
+                terms = ring.tile([P, BLOCKS, N], F32, name="terms")
+                nc.vector.tensor_scalar(
+                    terms[:], dist_cols[:], slope[:, h : h + 1], neg_shift_sbuf[:, h : h + 1], ALU.mult, ALU.max
                 )
-            for jb, h in vector_sums[len(vector_sums) * turn // H_TENSOR : len(vector_sums) * (turn + 1) // H_TENSOR]:
-                clipped_terms = unread.tile([P, N], F32, name="clipped_terms")
-                nc.vector.scalar_tensor_tensor(
-                    clipped_terms[:],
-                    dist_rows[jb][:],
-                    slope[:, h : h + 1],
-                    neg_shift[:, h : h + 1].to_broadcast([P, N]),
-                    ALU.mult,
-                    ALU.max,
-                    accum_out=clipped_sum[jb][:, h - H_SCALAR : h - H_SCALAR + 1],
-                )
-
-        for jb in range(BLOCKS):
-            nodes = slice(jb * P, (jb + 1) * P)
+                for kb in range(BLOCKS):
+                    nc.tensor.matmul(
+                        msg_sum[1][:],
+                        one_column[:, P - 1 - row : 2 * P - 1 - row],
+                        terms[:, kb, :],
+                        start=(jb == 0 and turn == 0 and kb == 0),
+                        stop=False,
+                    )
+                for i in range(H_VECTOR * turn // turns, H_VECTOR * (turn + 1) // turns):
+                    h = H_SCALAR + i
+                    clipped_terms = unread.tile([P, N], F32, name="clipped_terms")
+                    nc.vector.scalar_tensor_tensor(
+                        clipped_terms[:],
+                        dist_rows[jb][:],
+                        slope[:, h : h + 1],
+                        neg_shift[:, h : h + 1].to_broadcast([P, N]),
+                        ALU.mult,
+                        ALU.max,
+                        accum_out=clipped_sum[:, i : i + 1],
+                    )
             nc.vector.scalar_tensor_tensor(
-                msg_by_node[jb][:, H_SCALAR:C], shift[:, H_SCALAR:C], float(N), clipped_sum[jb][:], ALU.mult, ALU.add
+                msg_by_node[:, H_SCALAR:C], shift[:, H_SCALAR:C], float(N), clipped_sum[:], ALU.mult, ALU.add
             )
-            nc.tensor.matmul(msg_sum[0][:, nodes], msg_by_node[jb][:, 0:P], identity[:], start=(jb == 0), stop=(jb == 1))
-            nc.tensor.matmul(msg_sum[1][:, nodes], msg_by_node[jb][:, P:C], identity[:], start=False, stop=(jb == 1))
+
+            nc.tensor.matmul(msg_sum[0][:, nodes], msg_by_node[:, 0:P], identity[:], start=(jb == 0), stop=(jb == 1))
+            nc.tensor.matmul(msg_sum[1][:, nodes], msg_by_node[:, P:C], identity[:], start=False, stop=(jb == 1))
 
         msg = [held.tile([P, N], BF16, name=f"msg{hb}") for hb in range(BLOCKS)]
         nc.scalar.copy(msg[0][:], msg_sum[0][:])
@@ -142,7 +153,7 @@ def tile_s2v_dqn_kernel(tc, base, state, dist, w1, w4, b4, w3, bias, offs, out):
             total = work.tile([P, 1], F32, name="total")
             nc.scalar.activation(emb[:], emb_sum[:], ACT.Relu, accum_out=total[:])
             neg_mean = work.tile([P, 1], F32, name="neg_mean")
-            nc.vector.tensor_scalar_mul(neg_mean[:], total[:], -1.0 / N)
+            nc.scalar.mul(neg_mean[:], total[:], -1.0 / N)
             centered = work.tile([P, N], F32, name="centered")
             nc.vector.tensor_scalar_add(centered[:], emb[:], neg_mean[:])
             squares = work.tile([P, N], F32, name="squares")

@@ -10,9 +10,10 @@ C = 256
 N = 256
 S = 512
 BLOCKS = 2
+FLOAT_MAX = 3.4028234663852886e38
 
 H_SCALAR = 120
-H_VECTOR = 80
+H_VECTOR = 96
 H_TENSOR = C - H_SCALAR - H_VECTOR
 assert H_SCALAR % 8 == 0 and H_VECTOR % 8 == 0
 assert H_TENSOR <= P and H_TENSOR % BLOCKS == 0
@@ -60,8 +61,6 @@ def tile_s2v_dqn_kernel(tc, base, state, dist, w1, w4, b4, w3, bias, offs, out):
         nc.vector.memset(minus_ones[:], -1.0)
         neg_shift = psum_held.tile([P, C], F32, name="neg_shift")
         nc.tensor.matmul(neg_shift[:], minus_ones[:], b4_row[:], start=True, stop=True)
-        neg_shift_sbuf = held.tile([P, C], F32, name="neg_shift_sbuf")
-        nc.vector.tensor_scalar_mul(neg_shift_sbuf[:], shift[:], -1.0)
 
         own_weights = held.tile([2, C], F32, name="own_weights")
         nc.sync.dma_start(own_weights[0:1, :], bias.rearrange("c o -> o c"))
@@ -89,6 +88,7 @@ def tile_s2v_dqn_kernel(tc, base, state, dist, w1, w4, b4, w3, bias, offs, out):
         for jb in range(BLOCKS):
             nodes = slice(jb * P, (jb + 1) * P)
             msg_by_node = held.tile([P, C], F32, name=f"msg_by_node{jb}")
+            nc.gpsimd.memset(msg_by_node[:, C - H_TENSOR : C], 0.0)
 
             for h in range(H_SCALAR):
                 relu_terms = unread.tile([P, N], F32, name="relu_terms")
@@ -101,39 +101,40 @@ def tile_s2v_dqn_kernel(tc, base, state, dist, w1, w4, b4, w3, bias, offs, out):
                     accum_out=msg_by_node[:, h : h + 1],
                 )
 
-            clipped_sum = held.tile([P, C - H_SCALAR], F32, name=f"clipped_sum{jb}")
-            nc.gpsimd.memset(clipped_sum[:, H_VECTOR:], 0.0)
-            turns = H_TENSOR // BLOCKS
-            for turn in range(turns):
-                h = C - H_TENSOR + jb * turns + turn
+            clipped_sum = held.tile([P, H_VECTOR], F32, name=f"clipped_sum{jb}")
+            for i in range(H_VECTOR):
+                h = H_SCALAR + i
+                clipped_terms = unread.tile([P, N], F32, name="clipped_terms")
+                nc.vector.scalar_tensor_tensor(
+                    clipped_terms[:],
+                    dist_rows[jb][:],
+                    slope[:, h : h + 1],
+                    neg_shift[:, h : h + 1].to_broadcast([P, N]),
+                    ALU.mult,
+                    ALU.max,
+                    accum_out=clipped_sum[:, i : i + 1],
+                )
+            vector_channels = slice(H_SCALAR, H_SCALAR + H_VECTOR)
+            nc.vector.scalar_tensor_tensor(
+                msg_by_node[:, vector_channels], shift[:, vector_channels], float(N), clipped_sum[:], ALU.mult, ALU.add
+            )
+
+            for i in range(H_TENSOR // BLOCKS):
+                h = C - H_TENSOR + jb * (H_TENSOR // BLOCKS) + i
                 row = h - P
                 terms = ring.tile([P, BLOCKS, N], F32, name="terms")
-                nc.vector.tensor_scalar(
-                    terms[:], dist_cols[:], slope[:, h : h + 1], neg_shift_sbuf[:, h : h + 1], ALU.mult, ALU.max
+                nc.gpsimd.tensor_scalar(
+                    terms[:], dist_cols[:], slope[:, h : h + 1], shift[:, h : h + 1], ALU.mult, ALU.add
                 )
+                nc.gpsimd.tensor_scalar(terms[:], terms[:], FLOAT_MAX, 0.0, ALU.min, ALU.max)
                 for kb in range(BLOCKS):
                     nc.tensor.matmul(
                         msg_sum[1][:],
                         one_column[:, P - 1 - row : 2 * P - 1 - row],
                         terms[:, kb, :],
-                        start=(jb == 0 and turn == 0 and kb == 0),
+                        start=(jb == 0 and i == 0 and kb == 0),
                         stop=False,
                     )
-                for i in range(H_VECTOR * turn // turns, H_VECTOR * (turn + 1) // turns):
-                    h = H_SCALAR + i
-                    clipped_terms = unread.tile([P, N], F32, name="clipped_terms")
-                    nc.vector.scalar_tensor_tensor(
-                        clipped_terms[:],
-                        dist_rows[jb][:],
-                        slope[:, h : h + 1],
-                        neg_shift[:, h : h + 1].to_broadcast([P, N]),
-                        ALU.mult,
-                        ALU.max,
-                        accum_out=clipped_sum[:, i : i + 1],
-                    )
-            nc.vector.scalar_tensor_tensor(
-                msg_by_node[:, H_SCALAR:C], shift[:, H_SCALAR:C], float(N), clipped_sum[:], ALU.mult, ALU.add
-            )
 
             nc.tensor.matmul(msg_sum[0][:, nodes], msg_by_node[:, 0:P], identity[:], start=(jb == 0), stop=(jb == 1))
             nc.tensor.matmul(msg_sum[1][:, nodes], msg_by_node[:, P:C], identity[:], start=False, stop=(jb == 1))

@@ -13,9 +13,9 @@ BLOCKS = 2
 FLOAT_MAX = 3.4028234663852886e38
 
 H_SCALAR = 120
-H_VECTOR = 96
+H_VECTOR = 98
 H_TENSOR = C - H_SCALAR - H_VECTOR
-assert H_SCALAR % 8 == 0 and H_VECTOR % 8 == 0
+assert H_SCALAR % 8 == 0
 assert H_TENSOR <= P and H_TENSOR % BLOCKS == 0
 
 FLOPS = 4 * C * N * N + 2 * C * C * N
@@ -31,9 +31,6 @@ def tile_s2v_dqn_kernel(tc, base, state, dist, w1, w4, b4, w3, bias, offs, out):
         tc.psum_pool(name="psum", bufs=2) as psum,
         tc.psum_pool(name="psum_held", bufs=1) as psum_held,
     ):
-        offsets = held.tile([P, N // 16], U16, name="offsets")
-        nc.sync.dma_start(offsets[:], offs)
-
         dist_rows = [held.tile([P, N], F32, name=f"dist_rows{jb}") for jb in range(BLOCKS)]
         for jb in range(BLOCKS):
             nc.sync.dma_start(dist_rows[jb][:], dist[jb * P : (jb + 1) * P, :])
@@ -41,7 +38,10 @@ def tile_s2v_dqn_kernel(tc, base, state, dist, w1, w4, b4, w3, bias, offs, out):
         slope = held.tile([P, C], F32, name="slope")
         nc.scalar.dma_start(slope[:], w4.rearrange("h o -> (h o)").partition_broadcast(P))
         shift = held.tile([P, C], F32, name="shift")
-        nc.gpsimd.dma_start(shift[:], b4.rearrange("h o -> (h o)").partition_broadcast(P))
+        nc.scalar.dma_start(shift[:], b4.rearrange("h o -> (h o)").partition_broadcast(P))
+
+        offsets = held.tile([P, N // 16], U16, name="offsets")
+        nc.sync.dma_start(offsets[:], offs)
 
         scratch = held.tile([P, 1], F32, name="scratch")
         nc.vector.memset(scratch[:], 1.0)
@@ -87,8 +87,9 @@ def tile_s2v_dqn_kernel(tc, base, state, dist, w1, w4, b4, w3, bias, offs, out):
 
         for jb in range(BLOCKS):
             nodes = slice(jb * P, (jb + 1) * P)
+
             msg_by_node = held.tile([P, C], F32, name=f"msg_by_node{jb}")
-            nc.gpsimd.memset(msg_by_node[:, C - H_TENSOR : C], 0.0)
+            nc.vector.memset(msg_by_node[:, C - H_TENSOR : C], 0.0)
 
             for h in range(H_SCALAR):
                 relu_terms = unread.tile([P, N], F32, name="relu_terms")
@@ -136,7 +137,7 @@ def tile_s2v_dqn_kernel(tc, base, state, dist, w1, w4, b4, w3, bias, offs, out):
                         stop=False,
                     )
 
-            nc.tensor.matmul(msg_sum[0][:, nodes], msg_by_node[:, 0:P], identity[:], start=(jb == 0), stop=(jb == 1))
+            nc.tensor.transpose(msg_sum[0][:, nodes], msg_by_node[:, 0:P], identity[:])
             nc.tensor.matmul(msg_sum[1][:, nodes], msg_by_node[:, P:C], identity[:], start=False, stop=(jb == 1))
 
         msg = [held.tile([P, N], BF16, name=f"msg{hb}") for hb in range(BLOCKS)]

@@ -4,19 +4,19 @@ from concourse.masks import make_identity
 F32, BF16, U16 = mybir.dt.float32, mybir.dt.bfloat16, mybir.dt.uint16
 ACT = mybir.ActivationFunctionType
 ALU = mybir.AluOpType
+AXIS = mybir.AxisListType
 
 P = 128
 C = 256
 N = 256
 S = 512
 BLOCKS = 2
+PIECES = 3
+PLANES = PIECES + 1
 FLOAT_MAX = 3.4028234663852886e38
 
-H_SCALAR = 120
-H_VECTOR = 98
-H_TENSOR = C - H_SCALAR - H_VECTOR
-assert H_SCALAR % 8 == 0
-assert H_TENSOR <= P and H_TENSOR % BLOCKS == 0
+SHARE = 3
+LAG = 16
 
 FLOPS = 4 * C * N * N + 2 * C * C * N
 
@@ -25,8 +25,8 @@ def tile_s2v_dqn_kernel(tc, base, state, dist, w1, w4, b4, w3, bias, offs, out):
     nc = tc.nc
     with (
         tc.tile_pool(name="held", bufs=1) as held,
-        tc.tile_pool(name="unread", bufs=4) as unread,
-        tc.tile_pool(name="ring", bufs=4) as ring,
+        tc.tile_pool(name="vector_ring", bufs=16) as vector_ring,
+        tc.tile_pool(name="scalar_ring", bufs=8) as scalar_ring,
         tc.tile_pool(name="work", bufs=2) as work,
         tc.psum_pool(name="psum", bufs=2) as psum,
         tc.psum_pool(name="psum_held", bufs=1) as psum_held,
@@ -43,6 +43,11 @@ def tile_s2v_dqn_kernel(tc, base, state, dist, w1, w4, b4, w3, bias, offs, out):
         offsets = held.tile([P, N // 16], U16, name="offsets")
         nc.sync.dma_start(offsets[:], offs)
 
+        slope_col = held.tile([P, BLOCKS], F32, name="slope_col")
+        nc.sync.dma_start(slope_col[:], w4.rearrange("(a p) o -> p (a o)", p=P))
+        shift_col = held.tile([P, BLOCKS], F32, name="shift_col")
+        nc.sync.dma_start(shift_col[:], b4.rearrange("(a p) o -> p (a o)", p=P))
+
         scratch = held.tile([P, 1], F32, name="scratch")
         nc.vector.memset(scratch[:], 1.0)
         nc.scalar.activation(scratch[:], scratch[:], ACT.Sqrt)
@@ -51,16 +56,9 @@ def tile_s2v_dqn_kernel(tc, base, state, dist, w1, w4, b4, w3, bias, offs, out):
         make_identity(nc, identity[:])
         ones = held.tile([P, N], F32, name="ones")
         nc.gpsimd.memset(ones[:], 1.0)
-        one_column = held.tile([P, 2 * P - 1], F32, name="one_column")
-        nc.gpsimd.memset(one_column[:], 0.0)
-        nc.gpsimd.memset(one_column[:, P - 1 : P], 1.0)
 
-        b4_row = held.tile([1, C], F32, name="b4_row")
-        nc.sync.dma_start(b4_row[:], b4.rearrange("h o -> o h"))
-        minus_ones = held.tile([1, P], F32, name="minus_ones")
-        nc.vector.memset(minus_ones[:], -1.0)
-        neg_shift = psum_held.tile([P, C], F32, name="neg_shift")
-        nc.tensor.matmul(neg_shift[:], minus_ones[:], b4_row[:], start=True, stop=True)
+        planes = held.tile([P, PLANES, BLOCKS, N], BF16, name="planes")
+        nc.gpsimd.memset(planes[:, PIECES, :, :], 1.0)
 
         own_weights = held.tile([2, C], F32, name="own_weights")
         nc.sync.dma_start(own_weights[0:1, :], bias.rearrange("c o -> o c"))
@@ -76,73 +74,99 @@ def tile_s2v_dqn_kernel(tc, base, state, dist, w1, w4, b4, w3, bias, offs, out):
         for cb in range(BLOCKS):
             nc.sync.dma_start(window[cb][:], base[cb * P : (cb + 1) * P, :])
 
-        dist_cols = held.tile([P, BLOCKS, N], F32, name="dist_cols")
-        for jb in range(BLOCKS):
-            for kb in range(BLOCKS):
-                flipped = psum.tile([P, P], F32, name="flipped")
-                nc.tensor.transpose(flipped[:], dist_rows[jb][:, kb * P : (kb + 1) * P], identity[:])
-                nc.vector.tensor_copy(dist_cols[:, kb, jb * P : (jb + 1) * P], flipped[:])
+        inv_slope = held.tile([P, C], F32, name="inv_slope")
+        nc.vector.reciprocal(inv_slope[:], slope[:])
+        inv_finite = held.tile([P, C], F32, name="inv_finite")
+        nc.vector.tensor_scalar(inv_finite[:], inv_slope[:], FLOAT_MAX, -FLOAT_MAX, ALU.min, ALU.max)
+        quotient = held.tile([P, C], F32, name="quotient")
+        nc.vector.scalar_tensor_tensor(quotient[:], shift[:], -1.0, inv_finite[:], ALU.mult, ALU.mult)
+        threshold = held.tile([P, C], F32, name="threshold")
+        nc.vector.tensor_scalar(threshold[:], quotient[:], FLOAT_MAX, -FLOAT_MAX, ALU.min, ALU.max)
+        half_sign = held.tile([P, C], BF16, name="half_sign")
+        nc.vector.tensor_scalar(half_sign[:], inv_slope[:], 0.0, 0.5, ALU.is_ge, ALU.subtract)
 
-        msg_sum = [psum_held.tile([P, N], F32, name=f"msg_sum{hb}") for hb in range(BLOCKS)]
+        inv_col = held.tile([P, BLOCKS], F32, name="inv_col")
+        nc.vector.reciprocal(inv_col[:], slope_col[:])
+        half_sign_col = held.tile([P, BLOCKS], F32, name="half_sign_col")
+        nc.vector.tensor_scalar(half_sign_col[:], inv_col[:], 0.0, 0.5, ALU.is_ge, ALU.subtract)
+        abs_slope = held.tile([P, BLOCKS], F32, name="abs_slope")
+        nc.vector.scalar_tensor_tensor(abs_slope[:], slope_col[:], 2.0, half_sign_col[:], ALU.mult, ALU.mult)
+        signed_shift = held.tile([P, BLOCKS], F32, name="signed_shift")
+        nc.vector.scalar_tensor_tensor(signed_shift[:], shift_col[:], 2.0, half_sign_col[:], ALU.mult, ALU.mult)
+
+        dist_cols = held.tile([P, BLOCKS, N], F32, name="dist_cols")
+        rest = held.tile([P, BLOCKS, N], F32, name="rest")
+        half_planes = held.tile([P, PLANES, BLOCKS, N], BF16, name="half_planes")
+        for jb in range(BLOCKS):
+            nodes = slice(jb * P, (jb + 1) * P)
+            flipped = psum.tile([P, BLOCKS, P], F32, name="flipped")
+            for kb in range(BLOCKS):
+                nc.tensor.transpose(flipped[:, kb, :], dist_rows[jb][:, kb * P : (kb + 1) * P], identity[:])
+            nc.vector.tensor_copy(dist_cols[:, :, nodes], flipped[:])
+            nc.vector.tensor_copy(planes[:, 0, :, nodes], dist_cols[:, :, nodes])
+            nc.vector.tensor_tensor(rest[:, :, nodes], dist_cols[:, :, nodes], planes[:, 0, :, nodes], ALU.subtract)
+            nc.vector.tensor_copy(planes[:, 1, :, nodes], rest[:, :, nodes])
+            nc.vector.tensor_tensor(planes[:, 2, :, nodes], rest[:, :, nodes], planes[:, 1, :, nodes], ALU.subtract)
+            nc.vector.tensor_scalar_mul(half_planes[:, :, :, nodes], planes[:, :, :, nodes], 0.5)
+
+        msg = [held.tile([P, N], BF16, name=f"msg{hb}") for hb in range(BLOCKS)]
+        sums = [
+            [psum_held.tile([P, PLANES, P], F32, name=f"sums{jb}_{hb}") for hb in range(BLOCKS)]
+            for jb in range(BLOCKS)
+        ]
+
+        def finish_msg(jb):
+            nodes = slice(jb * P, (jb + 1) * P)
+            for hb in range(BLOCKS):
+                dist_sum = work.tile([P, P], F32, name="dist_sum")
+                nc.vector.tensor_reduce(
+                    dist_sum[:], sums[jb][hb][:, 0:PIECES, :].rearrange("p c j -> p j c"), AXIS.X, ALU.add
+                )
+                count_term = work.tile([P, P], F32, name="count_term")
+                nc.scalar.activation(
+                    count_term[:], sums[jb][hb][:, PIECES, :], ACT.Identity, scale=signed_shift[:, hb : hb + 1]
+                )
+                nc.vector.scalar_tensor_tensor(
+                    msg[hb][:, nodes], dist_sum[:], abs_slope[:, hb : hb + 1], count_term[:], ALU.mult, ALU.add
+                )
 
         for jb in range(BLOCKS):
             nodes = slice(jb * P, (jb + 1) * P)
-
-            msg_by_node = held.tile([P, C], F32, name=f"msg_by_node{jb}")
-            nc.vector.memset(msg_by_node[:, C - H_TENSOR : C], 0.0)
-
-            for h in range(H_SCALAR):
-                relu_terms = unread.tile([P, N], F32, name="relu_terms")
-                nc.scalar.activation(
-                    relu_terms[:],
-                    dist_rows[jb][:],
-                    ACT.Relu,
-                    bias=shift[:, h : h + 1],
-                    scale=slope[:, h : h + 1],
-                    accum_out=msg_by_node[:, h : h + 1],
-                )
-
-            clipped_sum = held.tile([P, H_VECTOR], F32, name=f"clipped_sum{jb}")
-            for i in range(H_VECTOR):
-                h = H_SCALAR + i
-                clipped_terms = unread.tile([P, N], F32, name="clipped_terms")
-                nc.vector.scalar_tensor_tensor(
-                    clipped_terms[:],
-                    dist_rows[jb][:],
-                    slope[:, h : h + 1],
-                    neg_shift[:, h : h + 1].to_broadcast([P, N]),
-                    ALU.mult,
-                    ALU.max,
-                    accum_out=clipped_sum[:, i : i + 1],
-                )
-            vector_channels = slice(H_SCALAR, H_SCALAR + H_VECTOR)
-            nc.vector.scalar_tensor_tensor(
-                msg_by_node[:, vector_channels], shift[:, vector_channels], float(N), clipped_sum[:], ALU.mult, ALU.add
-            )
-
-            for i in range(H_TENSOR // BLOCKS):
-                h = C - H_TENSOR + jb * (H_TENSOR // BLOCKS) + i
-                row = h - P
-                terms = ring.tile([P, BLOCKS, N], F32, name="terms")
-                nc.gpsimd.tensor_scalar(
-                    terms[:], dist_cols[:], slope[:, h : h + 1], shift[:, h : h + 1], ALU.mult, ALU.add
-                )
-                nc.gpsimd.tensor_scalar(terms[:], terms[:], FLOAT_MAX, 0.0, ALU.min, ALU.max)
+            for hb in range(BLOCKS):
                 for kb in range(BLOCKS):
                     nc.tensor.matmul(
-                        msg_sum[1][:],
-                        one_column[:, P - 1 - row : 2 * P - 1 - row],
-                        terms[:, kb, :],
-                        start=(jb == 0 and i == 0 and kb == 0),
+                        sums[jb][hb][:],
+                        half_sign[:, hb * P : (hb + 1) * P],
+                        planes[:, :, kb, nodes],
+                        start=(kb == 0),
                         stop=False,
                     )
-
-            nc.tensor.transpose(msg_sum[0][:, nodes], msg_by_node[:, 0:P], identity[:])
-            nc.tensor.matmul(msg_sum[1][:, nodes], msg_by_node[:, P:C], identity[:], start=False, stop=(jb == 1))
-
-        msg = [held.tile([P, N], BF16, name=f"msg{hb}") for hb in range(BLOCKS)]
-        nc.scalar.copy(msg[0][:], msg_sum[0][:])
-        nc.vector.tensor_copy(msg[1][:], msg_sum[1][:])
+            for i in range(P):
+                j = jb * P + i
+                if jb == 1 and i == LAG:
+                    finish_msg(0)
+                for kb in range(BLOCKS):
+                    if (BLOCKS * j + kb) % SHARE == SHARE - 1:
+                        side = scalar_ring.tile([P, C], BF16, name="side_by_scalar")
+                        nc.scalar.activation(
+                            side[:], threshold[:], ACT.Sign, bias=dist_cols[:, kb, j : j + 1], scale=-1.0
+                        )
+                        values = half_planes
+                    else:
+                        side = vector_ring.tile([P, C], BF16, name="side_by_vector")
+                        nc.vector.tensor_scalar(
+                            side[:], threshold[:], dist_cols[:, kb, j : j + 1], 0.5, ALU.is_lt, ALU.subtract
+                        )
+                        values = planes
+                    for hb in range(BLOCKS):
+                        nc.tensor.matmul(
+                            sums[jb][hb][:, :, i],
+                            side[:, hb * P : (hb + 1) * P],
+                            values[:, :, kb, j],
+                            start=False,
+                            stop=(i == P - 1 and kb == BLOCKS - 1),
+                        )
+        finish_msg(1)
 
         for cb in range(BLOCKS):
             channels = slice(cb * P, (cb + 1) * P)

@@ -13,6 +13,7 @@ S = 512
 BLOCKS = 2
 PIECES = 3
 PLANES = PIECES + 1
+STATS = 6
 FLOAT_MAX = 3.4028234663852886e38
 
 SHARE = 3
@@ -50,12 +51,10 @@ def tile_s2v_dqn_kernel(tc, base, state, dist, w1, w4, b4, w3, bias, offs, out):
 
         scratch = held.tile([P, 1], F32, name="scratch")
         nc.vector.memset(scratch[:], 1.0)
-        nc.scalar.activation(scratch[:], scratch[:], ACT.Sqrt)
+        nc.scalar.activation(scratch[:], scratch[:], ACT.Abs_reciprocal_sqrt)
 
         identity = held.tile([P, P], F32, name="identity")
         make_identity(nc, identity[:])
-        ones = held.tile([P, N], F32, name="ones")
-        nc.gpsimd.memset(ones[:], 1.0)
 
         planes = held.tile([P, PLANES, BLOCKS, N], BF16, name="planes")
         nc.gpsimd.memset(planes[:, PIECES, :, :], 1.0)
@@ -130,6 +129,20 @@ def tile_s2v_dqn_kernel(tc, base, state, dist, w1, w4, b4, w3, bias, offs, out):
                     msg[hb][:, nodes], dist_sum[:], abs_slope[:, hb : hb + 1], count_term[:], ALU.mult, ALU.add
                 )
 
+        emb_sum = [psum_held.tile([P, N], F32, name=f"emb_sum{cb}") for cb in range(BLOCKS)]
+        emb = [held.tile([P, N], F32, name=f"emb{cb}") for cb in range(BLOCKS)]
+        stats = [held.tile([P, BLOCKS, STATS], F32, name=f"stats{cb}") for cb in range(BLOCKS)]
+
+        def embed(jb):
+            nodes = slice(jb * P, (jb + 1) * P)
+            for cb in range(BLOCKS):
+                channels = slice(cb * P, (cb + 1) * P)
+                nc.tensor.matmul(emb_sum[cb][:, nodes], own_weights[:, channels], own_rows[:, nodes], start=True, stop=False)
+                nc.tensor.matmul(emb_sum[cb][:, nodes], w3_rows[0][:, channels], msg[0][:, nodes], start=False, stop=False)
+                nc.tensor.matmul(emb_sum[cb][:, nodes], w3_rows[1][:, channels], msg[1][:, nodes], start=False, stop=True)
+                nc.scalar.activation(emb[cb][:, nodes], emb_sum[cb][:, nodes], ACT.Relu)
+                nc.vector.bn_stats(stats[cb][:, jb, :], emb[cb][:, nodes])
+
         for jb in range(BLOCKS):
             nodes = slice(jb * P, (jb + 1) * P)
             for hb in range(BLOCKS):
@@ -145,6 +158,7 @@ def tile_s2v_dqn_kernel(tc, base, state, dist, w1, w4, b4, w3, bias, offs, out):
                 j = jb * P + i
                 if jb == 1 and i == LAG:
                     finish_msg(0)
+                    embed(0)
                 for kb in range(BLOCKS):
                     if (BLOCKS * j + kb) % SHARE == SHARE - 1:
                         side = scalar_ring.tile([P, C], BF16, name="side_by_scalar")
@@ -167,30 +181,18 @@ def tile_s2v_dqn_kernel(tc, base, state, dist, w1, w4, b4, w3, bias, offs, out):
                             stop=(i == P - 1 and kb == BLOCKS - 1),
                         )
         finish_msg(1)
+        embed(1)
 
         for cb in range(BLOCKS):
             channels = slice(cb * P, (cb + 1) * P)
-            emb_sum = psum.tile([P, N], F32, name="emb_sum")
-            nc.tensor.matmul(emb_sum[:], own_weights[:, channels], own_rows[:], start=True, stop=False)
-            nc.tensor.matmul(emb_sum[:], w3_rows[0][:, channels], msg[0][:], start=False, stop=False)
-            nc.tensor.matmul(emb_sum[:], w3_rows[1][:, channels], msg[1][:], start=False, stop=True)
-
-            emb = work.tile([P, N], F32, name="emb")
-            total = work.tile([P, 1], F32, name="total")
-            nc.scalar.activation(emb[:], emb_sum[:], ACT.Relu, accum_out=total[:])
-            neg_mean = work.tile([P, 1], F32, name="neg_mean")
-            nc.scalar.mul(neg_mean[:], total[:], -1.0 / N)
+            moments = work.tile([P, 2], F32, name="moments")
+            nc.vector.bn_aggr(moments[:], stats[cb][:].rearrange("p b s -> p (b s)"))
             centered = work.tile([P, N], F32, name="centered")
-            nc.vector.tensor_scalar_add(centered[:], emb[:], neg_mean[:])
-            squares = work.tile([P, N], F32, name="squares")
-            square_sum = work.tile([P, 1], F32, name="square_sum")
-            nc.scalar.activation(squares[:], emb[:], ACT.Square, bias=neg_mean[:], accum_out=square_sum[:])
-            std = work.tile([P, 1], F32, name="std")
-            nc.scalar.activation(std[:], square_sum[:], ACT.Sqrt, scale=1.0 / (N - 1))
-            inv_std = work.tile([P, 1], F32, name="inv_std")
-            nc.vector.reciprocal(inv_std[:], std[:])
+            nc.vector.tensor_scalar_sub(centered[:], emb[cb][:], moments[:, 0:1])
             inv_std_wide = work.tile([P, N], F32, name="inv_std_wide")
-            nc.vector.tensor_scalar_mul(inv_std_wide[:], ones[:], inv_std[:])
+            nc.scalar.activation(
+                inv_std_wide[:], moments[:, 1:2].to_broadcast([P, N]), ACT.Abs_reciprocal_sqrt, scale=float(N) / (N - 1)
+            )
 
             nc.vector.tensor_tensor(window[cb][:].indirect(offsets[:]), centered[:], inv_std_wide[:], ALU.mult)
             nc.sync.dma_start(out[channels, :], window[cb][:])

@@ -16,7 +16,8 @@ PLANES = PIECES + 1
 STATS = 6
 FLOAT_MAX = 3.4028234663852886e38
 
-SHARE = 3
+SCALAR_SHARE = 7
+SHARE_OF = 20
 LAG = 16
 
 FLOPS = 4 * C * N * N + 2 * C * C * N
@@ -160,7 +161,7 @@ def tile_s2v_dqn_kernel(tc, base, state, dist, w1, w4, b4, w3, bias, offs, out):
                     finish_msg(0)
                     embed(0)
                 for kb in range(BLOCKS):
-                    if (BLOCKS * j + kb) % SHARE == SHARE - 1:
+                    if ((BLOCKS * j + kb) * SCALAR_SHARE) % SHARE_OF < SCALAR_SHARE:
                         side = scalar_ring.tile([P, C], BF16, name="side_by_scalar")
                         nc.scalar.activation(
                             side[:], threshold[:], ACT.Sign, bias=dist_cols[:, kb, j : j + 1], scale=-1.0

@@ -18,7 +18,7 @@ FLOAT_MAX = 3.4028234663852886e38
 
 SCALAR_SHARE = 7
 SHARE_OF = 20
-LAG = 16
+LAG = 32
 
 FLOPS = 4 * C * N * N + 2 * C * C * N
 
@@ -27,8 +27,8 @@ def tile_s2v_dqn_kernel(tc, base, state, dist, w1, w4, b4, w3, bias, offs, out):
     nc = tc.nc
     with (
         tc.tile_pool(name="held", bufs=1) as held,
-        tc.tile_pool(name="vector_ring", bufs=16) as vector_ring,
-        tc.tile_pool(name="scalar_ring", bufs=8) as scalar_ring,
+        tc.tile_pool(name="vector_ring", bufs=32) as vector_ring,
+        tc.tile_pool(name="scalar_ring", bufs=16) as scalar_ring,
         tc.tile_pool(name="work", bufs=2) as work,
         tc.psum_pool(name="psum", bufs=2) as psum,
         tc.psum_pool(name="psum_held", bufs=1) as psum_held,

@@ -16,11 +16,19 @@ PLANES = PIECES + 1
 STATS = 6
 FLOAT_MAX = 3.4028234663852886e38
 
-SCALAR_SHARE = 7
-SHARE_OF = 20
+SCALAR_NODES = 45
+VECTOR_NODES = P - SCALAR_NODES
 LAG = 32
 
 FLOPS = 4 * C * N * N + 2 * C * C * N
+
+
+def in_turn(first, second):
+    order = []
+    for i, entry in enumerate(first):
+        order.append(entry)
+        order.extend(second[i * len(second) // len(first) : (i + 1) * len(second) // len(first)])
+    return order
 
 
 def tile_s2v_dqn_kernel(tc, base, state, dist, w1, w4, b4, w3, bias, offs, out):
@@ -82,21 +90,22 @@ def tile_s2v_dqn_kernel(tc, base, state, dist, w1, w4, b4, w3, bias, offs, out):
         nc.vector.scalar_tensor_tensor(quotient[:], shift[:], -1.0, inv_finite[:], ALU.mult, ALU.mult)
         threshold = held.tile([P, C], F32, name="threshold")
         nc.vector.tensor_scalar(threshold[:], quotient[:], FLOAT_MAX, -FLOAT_MAX, ALU.min, ALU.max)
-        half_sign = held.tile([P, C], BF16, name="half_sign")
-        nc.vector.tensor_scalar(half_sign[:], inv_slope[:], 0.0, 0.5, ALU.is_ge, ALU.subtract)
+        vector_lacks = held.tile([P, C], BF16, name="vector_lacks")
+        nc.vector.tensor_scalar(vector_lacks[:], inv_slope[:], 0.0, -2.0, ALU.is_lt, ALU.mult)
+        scalar_lacks = held.tile([P, C], BF16, name="scalar_lacks")
+        nc.vector.tensor_scalar_add(scalar_lacks[:], vector_lacks[:], 1.0)
 
         inv_col = held.tile([P, BLOCKS], F32, name="inv_col")
         nc.vector.reciprocal(inv_col[:], slope_col[:])
         half_sign_col = held.tile([P, BLOCKS], F32, name="half_sign_col")
         nc.vector.tensor_scalar(half_sign_col[:], inv_col[:], 0.0, 0.5, ALU.is_ge, ALU.subtract)
-        abs_slope = held.tile([P, BLOCKS], F32, name="abs_slope")
-        nc.vector.scalar_tensor_tensor(abs_slope[:], slope_col[:], 2.0, half_sign_col[:], ALU.mult, ALU.mult)
-        signed_shift = held.tile([P, BLOCKS], F32, name="signed_shift")
-        nc.vector.scalar_tensor_tensor(signed_shift[:], shift_col[:], 2.0, half_sign_col[:], ALU.mult, ALU.mult)
+        half_abs_slope = held.tile([P, BLOCKS], F32, name="half_abs_slope")
+        nc.vector.tensor_mul(half_abs_slope[:], slope_col[:], half_sign_col[:])
+        half_signed_shift = held.tile([P, BLOCKS], F32, name="half_signed_shift")
+        nc.vector.tensor_mul(half_signed_shift[:], shift_col[:], half_sign_col[:])
 
         dist_cols = held.tile([P, BLOCKS, N], F32, name="dist_cols")
         rest = held.tile([P, BLOCKS, N], F32, name="rest")
-        half_planes = held.tile([P, PLANES, BLOCKS, N], BF16, name="half_planes")
         for jb in range(BLOCKS):
             nodes = slice(jb * P, (jb + 1) * P)
             flipped = psum.tile([P, BLOCKS, P], F32, name="flipped")
@@ -107,7 +116,6 @@ def tile_s2v_dqn_kernel(tc, base, state, dist, w1, w4, b4, w3, bias, offs, out):
             nc.vector.tensor_tensor(rest[:, :, nodes], dist_cols[:, :, nodes], planes[:, 0, :, nodes], ALU.subtract)
             nc.vector.tensor_copy(planes[:, 1, :, nodes], rest[:, :, nodes])
             nc.vector.tensor_tensor(planes[:, 2, :, nodes], rest[:, :, nodes], planes[:, 1, :, nodes], ALU.subtract)
-            nc.vector.tensor_scalar_mul(half_planes[:, :, :, nodes], planes[:, :, :, nodes], 0.5)
 
         msg = [held.tile([P, N], BF16, name=f"msg{hb}") for hb in range(BLOCKS)]
         sums = [
@@ -124,10 +132,10 @@ def tile_s2v_dqn_kernel(tc, base, state, dist, w1, w4, b4, w3, bias, offs, out):
                 )
                 count_term = work.tile([P, P], F32, name="count_term")
                 nc.scalar.activation(
-                    count_term[:], sums[jb][hb][:, PIECES, :], ACT.Identity, scale=signed_shift[:, hb : hb + 1]
+                    count_term[:], sums[jb][hb][:, PIECES, :], ACT.Identity, scale=half_signed_shift[:, hb : hb + 1]
                 )
                 nc.vector.scalar_tensor_tensor(
-                    msg[hb][:, nodes], dist_sum[:], abs_slope[:, hb : hb + 1], count_term[:], ALU.mult, ALU.add
+                    msg[hb][:, nodes], dist_sum[:], half_abs_slope[:, hb : hb + 1], count_term[:], ALU.mult, ALU.add
                 )
 
         emb_sum = [psum_held.tile([P, N], F32, name=f"emb_sum{cb}") for cb in range(BLOCKS)]
@@ -144,42 +152,48 @@ def tile_s2v_dqn_kernel(tc, base, state, dist, w1, w4, b4, w3, bias, offs, out):
                 nc.scalar.activation(emb[cb][:, nodes], emb_sum[cb][:, nodes], ACT.Relu)
                 nc.vector.bn_stats(stats[cb][:, jb, :], emb[cb][:, nodes])
 
+        order = in_turn(list(range(VECTOR_NODES)), list(range(VECTOR_NODES, P)))
         for jb in range(BLOCKS):
-            nodes = slice(jb * P, (jb + 1) * P)
             for hb in range(BLOCKS):
+                channels = slice(hb * P, (hb + 1) * P)
                 for kb in range(BLOCKS):
                     nc.tensor.matmul(
-                        sums[jb][hb][:],
-                        half_sign[:, hb * P : (hb + 1) * P],
-                        planes[:, :, kb, nodes],
+                        sums[jb][hb][:, :, 0:VECTOR_NODES],
+                        vector_lacks[:, channels],
+                        planes[:, :, kb, jb * P : jb * P + VECTOR_NODES],
                         start=(kb == 0),
                         stop=False,
                     )
-            for i in range(P):
+                    nc.tensor.matmul(
+                        sums[jb][hb][:, :, VECTOR_NODES:P],
+                        scalar_lacks[:, channels],
+                        planes[:, :, kb, jb * P + VECTOR_NODES : (jb + 1) * P],
+                        start=False,
+                        stop=False,
+                    )
+            for place, i in enumerate(order):
                 j = jb * P + i
-                if jb == 1 and i == LAG:
+                if jb == 1 and place == LAG:
                     finish_msg(0)
                     embed(0)
                 for kb in range(BLOCKS):
-                    if ((BLOCKS * j + kb) * SCALAR_SHARE) % SHARE_OF < SCALAR_SHARE:
+                    if i < VECTOR_NODES:
+                        side = vector_ring.tile([P, C], BF16, name="side_by_vector")
+                        nc.vector.tensor_scalar(
+                            side[:], threshold[:], dist_cols[:, kb, j : j + 1], 2.0, ALU.is_lt, ALU.mult
+                        )
+                    else:
                         side = scalar_ring.tile([P, C], BF16, name="side_by_scalar")
                         nc.scalar.activation(
                             side[:], threshold[:], ACT.Sign, bias=dist_cols[:, kb, j : j + 1], scale=-1.0
                         )
-                        values = half_planes
-                    else:
-                        side = vector_ring.tile([P, C], BF16, name="side_by_vector")
-                        nc.vector.tensor_scalar(
-                            side[:], threshold[:], dist_cols[:, kb, j : j + 1], 0.5, ALU.is_lt, ALU.subtract
-                        )
-                        values = planes
                     for hb in range(BLOCKS):
                         nc.tensor.matmul(
                             sums[jb][hb][:, :, i],
                             side[:, hb * P : (hb + 1) * P],
-                            values[:, :, kb, j],
+                            planes[:, :, kb, j],
                             start=False,
-                            stop=(i == P - 1 and kb == BLOCKS - 1),
+                            stop=(place == P - 1 and kb == BLOCKS - 1),
                         )
         finish_msg(1)
         embed(1)

@@ -111,8 +111,12 @@ def tile_s2v_dqn_kernel(tc, base, state, dist, w1, w4, b4, w3, bias, offs, out):
             flipped = psum.tile([P, BLOCKS, P], F32, name="flipped")
             for kb in range(BLOCKS):
                 nc.tensor.transpose(flipped[:, kb, :], dist_rows[jb][:, kb * P : (kb + 1) * P], identity[:])
-            nc.vector.tensor_copy(dist_cols[:, :, nodes], flipped[:])
-            nc.vector.tensor_copy(planes[:, 0, :, nodes], dist_cols[:, :, nodes])
+            if jb == 0:
+                nc.vector.tensor_copy(dist_cols[:, :, nodes], flipped[:])
+                nc.scalar.activation(planes[:, 0, :, nodes], flipped[:], ACT.Identity)
+            else:
+                nc.scalar.activation(dist_cols[:, :, nodes], flipped[:], ACT.Identity)
+                nc.vector.tensor_copy(planes[:, 0, :, nodes], dist_cols[:, :, nodes])
             nc.vector.tensor_tensor(rest[:, :, nodes], dist_cols[:, :, nodes], planes[:, 0, :, nodes], ALU.subtract)
             nc.vector.tensor_copy(planes[:, 1, :, nodes], rest[:, :, nodes])
             nc.vector.tensor_tensor(planes[:, 2, :, nodes], rest[:, :, nodes], planes[:, 1, :, nodes], ALU.subtract)

@@ -108,14 +108,15 @@ def tile_s2v_dqn_kernel(tc, base, state, dist, w1, w4, b4, w3, bias, offs, out):
         rest = held.tile([P, BLOCKS, N], F32, name="rest")
         for jb in range(BLOCKS):
             nodes = slice(jb * P, (jb + 1) * P)
-            flipped = psum.tile([P, BLOCKS, P], F32, name="flipped")
             for kb in range(BLOCKS):
-                nc.tensor.transpose(flipped[:, kb, :], dist_rows[jb][:, kb * P : (kb + 1) * P], identity[:])
-            if jb == 0:
-                nc.vector.tensor_copy(dist_cols[:, :, nodes], flipped[:])
-                nc.scalar.activation(planes[:, 0, :, nodes], flipped[:], ACT.Identity)
-            else:
-                nc.scalar.activation(dist_cols[:, :, nodes], flipped[:], ACT.Identity)
+                flipped = psum.tile([P, P], F32, name="flipped")
+                nc.tensor.transpose(flipped[:], dist_rows[jb][:, kb * P : (kb + 1) * P], identity[:])
+                if jb == 0:
+                    nc.vector.tensor_copy(dist_cols[:, kb, nodes], flipped[:])
+                    nc.scalar.activation(planes[:, 0, kb, nodes], flipped[:], ACT.Identity)
+                else:
+                    nc.scalar.activation(dist_cols[:, kb, nodes], flipped[:], ACT.Identity)
+            if jb == 1:
                 nc.vector.tensor_copy(planes[:, 0, :, nodes], dist_cols[:, :, nodes])
             nc.vector.tensor_tensor(rest[:, :, nodes], dist_cols[:, :, nodes], planes[:, 0, :, nodes], ALU.subtract)
             nc.vector.tensor_copy(planes[:, 1, :, nodes], rest[:, :, nodes])

@@ -68,11 +68,13 @@ def tile_s2v_dqn_kernel(tc, base, state, dist, w1, w4, b4, w3, bias, offs, out):
         planes = held.tile([P, PLANES, BLOCKS, N], BF16, name="planes")
         nc.gpsimd.memset(planes[:, PIECES, :, :], 1.0)
 
-        own_weights = held.tile([2, C], F32, name="own_weights")
+        own_weights = held.tile([P, C], F32, name="own_weights")
+        nc.gpsimd.memset(own_weights[:], 0.0)
         nc.sync.dma_start(own_weights[0:1, :], bias.rearrange("c o -> o c"))
         nc.sync.dma_start(own_weights[1:2, :], w1.rearrange("c o -> o c"))
-        own_rows = held.tile([2, N], F32, name="own_rows")
-        nc.vector.memset(own_rows[0:1, :], 1.0)
+        own_rows = held.tile([P, N], F32, name="own_rows")
+        nc.gpsimd.memset(own_rows[:], 0.0)
+        nc.gpsimd.memset(own_rows[0:1, :], 1.0)
         nc.sync.dma_start(own_rows[1:2, :], state)
 
         w3_rows = [held.tile([P, C], BF16, name=f"w3_rows{hb}") for hb in range(BLOCKS)]

@@ -69,12 +69,12 @@ def tile_s2v_dqn_kernel(tc, base, state, dist, w1, w4, b4, w3, bias, offs, out):
         nc.gpsimd.memset(planes[:, PIECES, :, :], 1.0)
 
         own_weights = held.tile([P, C], F32, name="own_weights")
-        nc.gpsimd.memset(own_weights[:], 0.0)
+        nc.vector.memset(own_weights[:], 0.0)
         nc.sync.dma_start(own_weights[0:1, :], bias.rearrange("c o -> o c"))
         nc.sync.dma_start(own_weights[1:2, :], w1.rearrange("c o -> o c"))
         own_rows = held.tile([P, N], F32, name="own_rows")
-        nc.gpsimd.memset(own_rows[:], 0.0)
-        nc.gpsimd.memset(own_rows[0:1, :], 1.0)
+        nc.vector.memset(own_rows[:], 0.0)
+        nc.vector.memset(own_rows[0:1, :], 1.0)
         nc.sync.dma_start(own_rows[1:2, :], state)
 
         w3_rows = [held.tile([P, C], BF16, name=f"w3_rows{hb}") for hb in range(BLOCKS)]
@@ -111,15 +111,10 @@ def tile_s2v_dqn_kernel(tc, base, state, dist, w1, w4, b4, w3, bias, offs, out):
         for jb in range(BLOCKS):
             nodes = slice(jb * P, (jb + 1) * P)
             for kb in range(BLOCKS):
-                flipped = psum.tile([P, P], F32, name="flipped")
+                flipped = psum.tile([P, P], F32, name="flipped", tag="bank_in_turn")
                 nc.tensor.transpose(flipped[:], dist_rows[jb][:, kb * P : (kb + 1) * P], identity[:])
-                if jb == 0:
-                    nc.vector.tensor_copy(dist_cols[:, kb, nodes], flipped[:])
-                    nc.scalar.activation(planes[:, 0, kb, nodes], flipped[:], ACT.Identity)
-                else:
-                    nc.scalar.activation(dist_cols[:, kb, nodes], flipped[:], ACT.Identity)
-            if jb == 1:
-                nc.vector.tensor_copy(planes[:, 0, :, nodes], dist_cols[:, :, nodes])
+                nc.scalar.activation(dist_cols[:, kb, nodes], flipped[:], ACT.Identity)
+            nc.vector.tensor_copy(planes[:, 0, :, nodes], dist_cols[:, :, nodes])
             nc.vector.tensor_tensor(rest[:, :, nodes], dist_cols[:, :, nodes], planes[:, 0, :, nodes], ALU.subtract)
             nc.vector.tensor_copy(planes[:, 1, :, nodes], rest[:, :, nodes])
             nc.vector.tensor_tensor(planes[:, 2, :, nodes], rest[:, :, nodes], planes[:, 1, :, nodes], ALU.subtract)
@@ -145,7 +140,7 @@ def tile_s2v_dqn_kernel(tc, base, state, dist, w1, w4, b4, w3, bias, offs, out):
                     msg[hb][:, nodes], dist_sum[:], half_abs_slope[:, hb : hb + 1], count_term[:], ALU.mult, ALU.add
                 )
 
-        emb_sum = [psum_held.tile([P, N], F32, name=f"emb_sum{cb}") for cb in range(BLOCKS)]
+        emb_sum = [psum.tile([P, N], F32, name=f"emb_sum{cb}", tag="bank_in_turn") for cb in range(BLOCKS)]
         emb = [held.tile([P, N], F32, name=f"emb{cb}") for cb in range(BLOCKS)]
         stats = [held.tile([P, BLOCKS, STATS], F32, name=f"stats{cb}") for cb in range(BLOCKS)]
 

import concourse.mybir as mybir
from concourse.masks import make_identity

F32, BF16, U16 = mybir.dt.float32, mybir.dt.bfloat16, mybir.dt.uint16
ACT = mybir.ActivationFunctionType
ALU = mybir.AluOpType
AXIS = mybir.AxisListType

P = 128
C = 256
N = 256
S = 512
BLOCKS = 2
PIECES = 3
PLANES = PIECES + 1
STATS = 6
FLOAT_MAX = 3.4028234663852886e38

SCALAR_NODES = 45
VECTOR_NODES = P - SCALAR_NODES
LAG = 32

FLOPS = 4 * C * N * N + 2 * C * C * N


def in_turn(first, second):
    order = []
    for i, entry in enumerate(first):
        order.append(entry)
        order.extend(second[i * len(second) // len(first) : (i + 1) * len(second) // len(first)])
    return order


def tile_s2v_dqn_kernel(tc, base, state, dist, w1, w4, b4, w3, bias, offs, out):
    nc = tc.nc
    with (
        tc.tile_pool(name="held", bufs=1) as held,
        tc.tile_pool(name="vector_ring", bufs=32) as vector_ring,
        tc.tile_pool(name="scalar_ring", bufs=16) as scalar_ring,
        tc.tile_pool(name="work", bufs=2) as work,
        tc.psum_pool(name="psum", bufs=2) as psum,
        tc.psum_pool(name="psum_held", bufs=1) as psum_held,
    ):
        dist_rows = [held.tile([P, N], F32, name=f"dist_rows{jb}") for jb in range(BLOCKS)]
        for jb in range(BLOCKS):
            nc.sync.dma_start(dist_rows[jb][:], dist[jb * P : (jb + 1) * P, :])

        slope = held.tile([P, C], F32, name="slope")
        nc.scalar.dma_start(slope[:], w4.rearrange("h o -> (h o)").partition_broadcast(P))
        shift = held.tile([P, C], F32, name="shift")
        nc.scalar.dma_start(shift[:], b4.rearrange("h o -> (h o)").partition_broadcast(P))

        offsets = held.tile([P, N // 16], U16, name="offsets")
        nc.sync.dma_start(offsets[:], offs)

        slope_col = held.tile([P, BLOCKS], F32, name="slope_col")
        nc.sync.dma_start(slope_col[:], w4.rearrange("(a p) o -> p (a o)", p=P))
        shift_col = held.tile([P, BLOCKS], F32, name="shift_col")
        nc.sync.dma_start(shift_col[:], b4.rearrange("(a p) o -> p (a o)", p=P))

        scratch = held.tile([P, 1], F32, name="scratch")
        nc.vector.memset(scratch[:], 1.0)
        nc.scalar.activation(scratch[:], scratch[:], ACT.Abs_reciprocal_sqrt)

        identity = held.tile([P, P], F32, name="identity")
        make_identity(nc, identity[:])

        planes = held.tile([P, PLANES, BLOCKS, N], BF16, name="planes")
        nc.gpsimd.memset(planes[:, PIECES, :, :], 1.0)

        own_weights = held.tile([P, C], F32, name="own_weights")
        nc.vector.memset(own_weights[:], 0.0)
        nc.sync.dma_start(own_weights[0:1, :], bias.rearrange("c o -> o c"))
        nc.sync.dma_start(own_weights[1:2, :], w1.rearrange("c o -> o c"))
        own_rows = held.tile([P, N], F32, name="own_rows")
        nc.vector.memset(own_rows[:], 0.0)
        nc.vector.memset(own_rows[0:1, :], 1.0)
        nc.sync.dma_start(own_rows[1:2, :], state)

        w3_rows = [held.tile([P, C], BF16, name=f"w3_rows{hb}") for hb in range(BLOCKS)]
        for hb in range(BLOCKS):
            nc.sync.dma_start(w3_rows[hb][:], w3[hb * P : (hb + 1) * P, :])
        window = [held.tile([P, S], F32, name=f"window{cb}") for cb in range(BLOCKS)]
        for cb in range(BLOCKS):
            nc.sync.dma_start(window[cb][:], base[cb * P : (cb + 1) * P, :])

        inv_slope = held.tile([P, C], F32, name="inv_slope")
        nc.vector.reciprocal(inv_slope[:], slope[:])
        inv_finite = held.tile([P, C], F32, name="inv_finite")
        nc.vector.tensor_scalar(inv_finite[:], inv_slope[:], FLOAT_MAX, -FLOAT_MAX, ALU.min, ALU.max)
        quotient = held.tile([P, C], F32, name="quotient")
        nc.vector.scalar_tensor_tensor(quotient[:], shift[:], -1.0, inv_finite[:], ALU.mult, ALU.mult)
        threshold = held.tile([P, C], F32, name="threshold")
        nc.vector.tensor_scalar(threshold[:], quotient[:], FLOAT_MAX, -FLOAT_MAX, ALU.min, ALU.max)
        vector_lacks = held.tile([P, C], BF16, name="vector_lacks")
        nc.vector.tensor_scalar(vector_lacks[:], inv_slope[:], 0.0, -2.0, ALU.is_lt, ALU.mult)
        scalar_lacks = held.tile([P, C], BF16, name="scalar_lacks")
        nc.vector.tensor_scalar_add(scalar_lacks[:], vector_lacks[:], 1.0)

        inv_col = held.tile([P, BLOCKS], F32, name="inv_col")
        nc.vector.reciprocal(inv_col[:], slope_col[:])
        half_sign_col = held.tile([P, BLOCKS], F32, name="half_sign_col")
        nc.vector.tensor_scalar(half_sign_col[:], inv_col[:], 0.0, 0.5, ALU.is_ge, ALU.subtract)
        half_abs_slope = held.tile([P, BLOCKS], F32, name="half_abs_slope")
        nc.vector.tensor_mul(half_abs_slope[:], slope_col[:], half_sign_col[:])
        half_signed_shift = held.tile([P, BLOCKS], F32, name="half_signed_shift")
        nc.vector.tensor_mul(half_signed_shift[:], shift_col[:], half_sign_col[:])

        dist_cols = held.tile([P, BLOCKS, N], F32, name="dist_cols")
        rest = held.tile([P, BLOCKS, N], F32, name="rest")
        for jb in range(BLOCKS):
            nodes = slice(jb * P, (jb + 1) * P)
            for kb in range(BLOCKS):
                flipped = psum.tile([P, P], F32, name="flipped", tag="bank_in_turn")
                nc.tensor.transpose(flipped[:], dist_rows[jb][:, kb * P : (kb + 1) * P], identity[:])
                nc.scalar.activation(dist_cols[:, kb, nodes], flipped[:], ACT.Identity)
            nc.vector.tensor_copy(planes[:, 0, :, nodes], dist_cols[:, :, nodes])
            nc.vector.tensor_tensor(rest[:, :, nodes], dist_cols[:, :, nodes], planes[:, 0, :, nodes], ALU.subtract)
            nc.vector.tensor_copy(planes[:, 1, :, nodes], rest[:, :, nodes])
            nc.vector.tensor_tensor(planes[:, 2, :, nodes], rest[:, :, nodes], planes[:, 1, :, nodes], ALU.subtract)

        msg = [held.tile([P, N], BF16, name=f"msg{hb}") for hb in range(BLOCKS)]
        sums = [
            [psum_held.tile([P, PLANES, P], F32, name=f"sums{jb}_{hb}") for hb in range(BLOCKS)]
            for jb in range(BLOCKS)
        ]

        def finish_msg(jb):
            nodes = slice(jb * P, (jb + 1) * P)
            for hb in range(BLOCKS):
                dist_sum = work.tile([P, P], F32, name="dist_sum")
                nc.vector.tensor_reduce(
                    dist_sum[:], sums[jb][hb][:, 0:PIECES, :].rearrange("p c j -> p j c"), AXIS.X, ALU.add
                )
                count_term = work.tile([P, P], F32, name="count_term")
                nc.scalar.activation(
                    count_term[:], sums[jb][hb][:, PIECES, :], ACT.Identity, scale=half_signed_shift[:, hb : hb + 1]
                )
                nc.vector.scalar_tensor_tensor(
                    msg[hb][:, nodes], dist_sum[:], half_abs_slope[:, hb : hb + 1], count_term[:], ALU.mult, ALU.add
                )

        emb_sum = [psum.tile([P, N], F32, name=f"emb_sum{cb}", tag="bank_in_turn") for cb in range(BLOCKS)]
        emb = [held.tile([P, N], F32, name=f"emb{cb}") for cb in range(BLOCKS)]
        stats = [held.tile([P, BLOCKS, STATS], F32, name=f"stats{cb}") for cb in range(BLOCKS)]

        def embed(jb):
            nodes = slice(jb * P, (jb + 1) * P)
            for cb in range(BLOCKS):
                channels = slice(cb * P, (cb + 1) * P)
                nc.tensor.matmul(emb_sum[cb][:, nodes], own_weights[:, channels], own_rows[:, nodes], start=True, stop=False)
                nc.tensor.matmul(emb_sum[cb][:, nodes], w3_rows[0][:, channels], msg[0][:, nodes], start=False, stop=False)
                nc.tensor.matmul(emb_sum[cb][:, nodes], w3_rows[1][:, channels], msg[1][:, nodes], start=False, stop=True)
                nc.scalar.activation(emb[cb][:, nodes], emb_sum[cb][:, nodes], ACT.Relu)
                nc.vector.bn_stats(stats[cb][:, jb, :], emb[cb][:, nodes])

        order = in_turn(list(range(VECTOR_NODES)), list(range(VECTOR_NODES, P)))
        for jb in range(BLOCKS):
            for hb in range(BLOCKS):
                channels = slice(hb * P, (hb + 1) * P)
                for kb in range(BLOCKS):
                    nc.tensor.matmul(
                        sums[jb][hb][:, :, 0:VECTOR_NODES],
                        vector_lacks[:, channels],
                        planes[:, :, kb, jb * P : jb * P + VECTOR_NODES],
                        start=(kb == 0),
                        stop=False,
                    )
                    nc.tensor.matmul(
                        sums[jb][hb][:, :, VECTOR_NODES:P],
                        scalar_lacks[:, channels],
                        planes[:, :, kb, jb * P + VECTOR_NODES : (jb + 1) * P],
                        start=False,
                        stop=False,
                    )
            for place, i in enumerate(order):
                j = jb * P + i
                if jb == 1 and place == LAG:
                    finish_msg(0)
                    embed(0)
                for kb in range(BLOCKS):
                    if i < VECTOR_NODES:
                        side = vector_ring.tile([P, C], BF16, name="side_by_vector")
                        nc.vector.tensor_scalar(
                            side[:], threshold[:], dist_cols[:, kb, j : j + 1], 2.0, ALU.is_lt, ALU.mult
                        )
                    else:
                        side = scalar_ring.tile([P, C], BF16, name="side_by_scalar")
                        nc.scalar.activation(
                            side[:], threshold[:], ACT.Sign, bias=dist_cols[:, kb, j : j + 1], scale=-1.0
                        )
                    for hb in range(BLOCKS):
                        nc.tensor.matmul(
                            sums[jb][hb][:, :, i],
                            side[:, hb * P : (hb + 1) * P],
                            planes[:, :, kb, j],
                            start=False,
                            stop=(place == P - 1 and kb == BLOCKS - 1),
                        )
        finish_msg(1)
        embed(1)

        for cb in range(BLOCKS):
            channels = slice(cb * P, (cb + 1) * P)
            moments = work.tile([P, 2], F32, name="moments")
            nc.vector.bn_aggr(moments[:], stats[cb][:].rearrange("p b s -> p (b s)"))
            centered = work.tile([P, N], F32, name="centered")
            nc.vector.tensor_scalar_sub(centered[:], emb[cb][:], moments[:, 0:1])
            inv_std_wide = work.tile([P, N], F32, name="inv_std_wide")
            nc.scalar.activation(
                inv_std_wide[:], moments[:, 1:2].to_broadcast([P, N]), ACT.Abs_reciprocal_sqrt, scale=float(N) / (N - 1)
            )

            nc.vector.tensor_tensor(window[cb][:].indirect(offsets[:]), centered[:], inv_std_wide[:], ALU.mult)
            nc.sync.dma_start(out[channels, :], window[cb][:])
